import numpy as np
import ml_dtypes


def mxq(x, axis, fmt="e4m3"):
    dtype, down = {"e4m3": (ml_dtypes.float8_e4m3fn, 7), "e5m2": (ml_dtypes.float8_e5m2, 14)}[fmt]
    v = np.moveaxis(np.asarray(x, np.float32).astype(ml_dtypes.bfloat16).astype(np.float64), axis, -1)
    blocks = v.reshape(v.shape[:-1] + (-1, 32))
    amax = np.abs(blocks).max(-1, keepdims=True)
    byte = np.maximum(np.where(amax > 0, np.frexp(amax)[1] - 1 + 127, 0) - down, 1)
    scale = np.exp2(byte - 127.0)
    codes = (blocks / scale).astype(np.float32).astype(dtype).astype(np.float64)
    return np.moveaxis((codes * scale).reshape(v.shape), -1, axis)


WIDE = False


def mx_kscale(k):
    if not WIDE:
        return np.ones(k)
    levels = np.array([10, -10, 5, -5, 0])
    if k % 512:
        return np.exp2(np.random.permutation(np.resize(levels, k // 32))).repeat(32)
    a = np.empty((k // 512, 16))
    for p in range(k // 512):
        a[p, :8] = np.random.permutation(np.resize(levels, 8))
        for g in range(8):
            far = levels[np.abs(levels - a[p, g]) >= 10]
            a[p, g + 8] = far[np.random.randint(len(far))]
    return np.exp2(a.ravel()).repeat(32)


BF16 = ml_dtypes.bfloat16


def bf(x):
    return np.asarray(x, np.float32).astype(BF16)


def f64(x):
    return np.asarray(x).astype(np.float64)


B, D_IN, D_H = 512, 1024, 1024


def sigmoid(v):
    return 1.0 / (1.0 + np.exp(-v))


def setup_inputs():
    s, t = mx_kscale(D_IN), mx_kscale(D_H)

    def w_in():
        return bf(np.random.standard_normal((D_H, D_IN)) * 0.6 / np.sqrt(D_IN) / s[None, :])

    def w_rec():
        return bf(np.random.standard_normal((D_H, D_H)) * 0.6 / np.sqrt(D_H) / t[None, :])

    def bias():
        return bf(np.random.standard_normal(D_H) * 0.3)

    return {"incoming": bf(np.random.standard_normal((B, D_IN)) * s), "h": bf(np.random.standard_normal((B, D_H)) * t),
            "c": bf(np.random.standard_normal((B, D_H))), "gated_cand": bf(np.random.standard_normal((B, D_H)) * 0.5),
            "W_f": w_in(), "b_W_f": bias(), "W_o": w_in(), "b_W_o": bias(),
            "U_f": w_rec(), "b_U_f": bias(), "U_o": w_rec(), "b_U_o": bias()}


def reference(incoming, h, c, gated_cand, W_f, b_W_f, W_o, b_W_o, U_f, b_U_f, U_o, b_U_o):
    xq = mxq(f64(incoming), 1, "e4m3")
    hq = mxq(f64(h), 1, "e4m3")
    O = sigmoid((xq @ mxq(f64(W_o), 1, "e4m3").T) + f64(b_W_o) + (hq @ mxq(f64(U_o), 1, "e4m3").T) + f64(b_U_o))
    F = sigmoid((xq @ mxq(f64(W_f), 1, "e4m3").T) + f64(b_W_f) + (hq @ mxq(f64(U_f), 1, "e4m3").T) + f64(b_U_f))
    C = F * f64(c) + f64(gated_cand)
    H = O * np.tanh(C)
    return (H, C)

@@ -1,0 +1,220 @@
+from contextlib import ExitStack
+
+import concourse.mybir as mybir
+from concourse.masks import make_identity
+
+F32 = mybir.dt.float32
+BF16 = mybir.dt.bfloat16
+U32 = mybir.dt.uint32
+U8 = mybir.dt.uint8
+FP8X4 = mybir.dt.float8_e4m3fn_x4
+ACT = mybir.ActivationFunctionType
+ALU = mybir.AluOpType
+
+P = 128
+BATCH = 512
+FEATURES = 1024
+PACK = 4
+K_PASS = P * PACK
+PASSES = FEATURES // K_PASS
+PAIRS = 2
+SOURCES = 2
+GATES = 2
+BATCH_TILES = BATCH // P
+WIDTH = 256
+ROUNDS_PER_GATE = FEATURES // WIDTH
+ROUNDS = GATES * ROUNDS_PER_GATE
+BLOCKS = 4
+BANK = 512
+ROWS_PER_RUN = 2
+TILES_PER_BANK = BANK // WIDTH
+BANKS = BATCH_TILES // TILES_PER_BANK
+HEAD_UNITS = 3
+SHARED_COPIES = 2
+
+MULTIPLY_LAG = 1
+SIGMOID_LAG = 2
+SUM_LAG = 3
+TANH_LAG = 4
+
+FLOPS = 2 * BATCH * (SOURCES * FEATURES) * (GATES * FEATURES)
+
+
+def tile_lstmcell_pb_kernel(
+    tc, incoming, h, c, gated_cand, W_f, b_W_f, W_o, b_W_o, U_f, b_U_f, U_o, b_U_o, out_0, out_1
+):
+    nc = tc.nc
+    with ExitStack() as ctx:
+        const = ctx.enter_context(tc.tile_pool(name="const", bufs=1))
+        raw_pool = ctx.enter_context(tc.tile_pool(name="raw", bufs=1))
+        grouped_pool = ctx.enter_context(tc.tile_pool(name="grouped", bufs=3))
+        act_pool = ctx.enter_context(tc.tile_pool(name="act", bufs=SOURCES))
+        weight_pool = ctx.enter_context(tc.tile_pool(name="weight", bufs=3))
+        gate_pool = ctx.enter_context(tc.tile_pool(name="gate", bufs=10))
+        cell_pool = ctx.enter_context(tc.tile_pool(name="cell", bufs=8))
+        tanh_pool = ctx.enter_context(tc.tile_pool(name="tanh", bufs=8))
+        transposed = ctx.enter_context(tc.psum_pool(name="transposed", bufs=4))
+        sums = ctx.enter_context(tc.psum_pool(name="sums", bufs=4))
+        ctx.enter_context(tc.manual_schedule())
+
+        ident = const.tile([P, P], F32, name="ident")
+        make_identity(nc, ident[:])
+        ones = const.tile([P, P], BF16, name="ones")
+        nc.vector.memset(ones[:], 1.0)
+        warm = const.tile([P, 1], F32, name="warm")
+        nc.vector.memset(warm[:], 0.0)
+        nc.scalar.activation(out=warm[:], in_=warm[:], func=ACT.Sigmoid)
+        bias_rows = const.tile([P, GATES * FEATURES], BF16, name="bias_rows")
+        nc.vector.memset(bias_rows[:], 0.0)
+        for gate, pair in enumerate(((b_W_f, b_U_f), (b_W_o, b_U_o))):
+            for row, vector in enumerate(pair):
+                nc.scalar.dma_start(
+                    out=bias_rows[row : row + 1, gate * FEATURES : (gate + 1) * FEATURES],
+                    in_=vector.rearrange("(o n) -> o n", o=1),
+                )
+
+        gate_weights = ((W_f, U_f), (W_o, U_o))
+        units = []
+        for name, matrix in (("x", incoming), ("h", h)):
+            by_tile = matrix.rearrange("(p b) k -> p b k", b=BATCH_TILES)
+            loads = [by_tile[:, a * ROWS_PER_RUN : (a + 1) * ROWS_PER_RUN, :] for a in range(BLOCKS // ROWS_PER_RUN)]
+            blocks = [{"slot": 0, "column": i * P} for i in range(BLOCKS)]
+            units.append({"name": name, "loads": loads, "blocks": blocks, "slots": PASSES})
+        for number in range(ROUNDS):
+            gate, part = divmod(number, ROUNDS_PER_GATE)
+            rows = slice(part * WIDTH, (part + 1) * WIDTH)
+            loads = [gate_weights[gate][source][rows, :].rearrange("(p t) k -> p t k", t=ROWS_PER_RUN) for source in range(SOURCES)]
+            blocks = [{"slot": source * PASSES, "column": t * P} for source in range(SOURCES) for t in range(ROWS_PER_RUN)]
+            units.append({"name": "r%d" % number, "loads": loads, "blocks": blocks, "slots": SOURCES * PASSES})
+        first_round = len(units) - ROUNDS
+
+        c_sb = raw_pool.tile([P, BATCH_TILES, FEATURES], BF16, name="c_sb")
+        g_sb = raw_pool.tile([P, BATCH_TILES, FEATURES], BF16, name="g_sb")
+        for index, unit in enumerate(units):
+            for a, rows in enumerate(unit["loads"]):
+                raw = raw_pool.tile([P, ROWS_PER_RUN, FEATURES], BF16, name="raw_%s_%d" % (unit["name"], a))
+                nc.sync.dma_start(out=raw[:], in_=rows)
+                for t in range(ROWS_PER_RUN):
+                    unit["blocks"][a * ROWS_PER_RUN + t]["raw"] = raw[:, t, :]
+            if index == first_round + 1:
+                nc.sync.dma_start(out=c_sb[:], in_=c.rearrange("(p b) n -> p b n", b=BATCH_TILES))
+            if index == first_round + 2:
+                nc.sync.dma_start(out=g_sb[:], in_=gated_cand.rearrange("(p b) n -> p b n", b=BATCH_TILES))
+
+        def transpose_unit(unit, vector_copies):
+            grouped = grouped_pool.tile([P, BLOCKS * FEATURES], BF16, name="grouped", align_bytes=64)
+            grouped_words = grouped[:].bitcast(F32).rearrange("p (s r u) -> p s r u", s=unit["slots"], u=PAIRS)
+            for i, block in enumerate(unit["blocks"]):
+                raw_words = block["raw"].bitcast(F32)
+                bank = transposed.tile([P, PASSES, PAIRS, P], F32, name="bank")
+                for g in range(PASSES):
+                    for u in range(PAIRS):
+                        words = slice(g * K_PASS // 2 + u, (g + 1) * K_PASS // 2, PAIRS)
+                        nc.tensor.transpose(bank[:, g, u, :], raw_words[:, words], ident[:])
+                copy_out = nc.vector.tensor_copy if i >= BLOCKS - vector_copies else nc.scalar.copy
+                copy_out(
+                    out=grouped_words[:, block["slot"] : block["slot"] + PASSES, block["column"] : block["column"] + P, :],
+                    in_=bank[:].rearrange("p g u r -> p g r u"),
+                )
+            unit["grouped"] = grouped
+
+        def quantise_unit(unit, pool):
+            codes = pool.tile([P, BLOCKS * FEATURES // PACK], U32, name="codes", align_bytes=64)
+            scales = pool.tile([P, BLOCKS * FEATURES // PACK], U8, name="scales", align_bytes=64)
+            nc.vector.quantize_mx(out=codes[:].bitcast(FP8X4), scales=scales[:], in_=unit["grouped"][:])
+            unit["codes"] = codes
+            unit["scales"] = scales
+
+        def multiply_round(unit):
+            unit["sums"] = []
+            for t in range(BANKS):
+                bank = sums.tile([P, TILES_PER_BANK, WIDTH], F32, name="sum")
+                for j in range(TILES_PER_BANK):
+                    b = t * TILES_PER_BANK + j
+                    for slot in range(SOURCES * PASSES):
+                        source, g = divmod(slot, PASSES)
+                        m_cols = slice(g * BATCH + b * P, g * BATCH + (b + 1) * P)
+                        n_cols = slice(slot * WIDTH, (slot + 1) * WIDTH)
+                        nc.tensor.matmul_mx(
+                            out=bank[:, j, :],
+                            lhsT=units[source]["codes"][:, m_cols].bitcast(FP8X4),
+                            lhsT_scale=units[source]["scales"][:, m_cols],
+                            rhs=unit["codes"][:, n_cols].bitcast(FP8X4),
+                            rhs_scale=unit["scales"][:, n_cols],
+                            start=(slot == 0),
+                            stop=(slot == SOURCES * PASSES - 1),
+                        )
+                unit["sums"].append(bank)
+
+        def round_at(step, lag):
+            number = step - lag - first_round
+            return number if 0 <= number < ROUNDS else None
+
+        def rows_of(t):
+            return slice(t * TILES_PER_BANK, (t + 1) * TILES_PER_BANK)
+
+        bias_sb = const.tile([P, GATES * FEATURES], F32, name="bias_sb")
+        out_h = out_0.rearrange("(p b) n -> p b n", b=BATCH_TILES)
+        out_c = out_1.rearrange("(p b) n -> p b n", b=BATCH_TILES)
+        gates = {}
+        cells = {}
+        tanhs = {}
+
+        for step in range(len(units) + SIGMOID_LAG):
+            if step < len(units):
+                transpose_unit(units[step], SHARED_COPIES if step < HEAD_UNITS else 0)
+            for q in range(GATES * FEATURES // BANK):
+                if step == 1 + q // (FEATURES // BANK):
+                    bank = sums.tile([P, BANK], F32, name="sum")
+                    nc.tensor.matmul(out=bank[:], lhsT=ones[:], rhs=bias_rows[:, q * BANK : (q + 1) * BANK], start=True, stop=True)
+                    nc.scalar.copy(out=bias_sb[:, q * BANK : (q + 1) * BANK], in_=bank[:])
+
+            number = round_at(step, SIGMOID_LAG)
+            if number is not None:
+                for t in range(BANKS):
+                    nc.scalar.activation(out=gates[number][t][:], in_=gates[number][t][:], func=ACT.Sigmoid)
+
+            number = round_at(step, TANH_LAG)
+            if number is not None and number < ROUNDS_PER_GATE:
+                cols = slice(number * WIDTH, (number + 1) * WIDTH)
+                tanhs[number] = [tanh_pool.tile([P, TILES_PER_BANK, WIDTH], F32, name="tanh_c") for t in range(BANKS)]
+                for t in range(BANKS):
+                    nc.scalar.activation(out=tanhs[number][t][:], in_=cells[number][t][:], func=ACT.Tanh)
+                    nc.sync.dma_start(out=out_c[:, rows_of(t), cols], in_=cells[number][t][:])
+
+            number = round_at(step, SUM_LAG)
+            if number is not None and number < ROUNDS_PER_GATE:
+                cols = slice(number * WIDTH, (number + 1) * WIDTH)
+                cells[number] = [cell_pool.tile([P, TILES_PER_BANK, WIDTH], F32, name="cell") for t in range(BANKS)]
+                for t in range(BANKS):
+                    nc.vector.tensor_tensor(out=cells[number][t][:], in0=gates[number][t][:], in1=g_sb[:, rows_of(t), cols], op=ALU.add)
+
+            number = round_at(step, MULTIPLY_LAG)
+            if number is not None:
+                multiply_round(units[first_round + number])
+
+            if step < len(units):
+                quantise_unit(units[step], act_pool if step < first_round else weight_pool)
+
+            if number is not None:
+                bias_cols = bias_sb[:, number * WIDTH : (number + 1) * WIDTH].rearrange("p (r t) -> p r t", t=ROWS_PER_RUN)
+                gates[number] = [gate_pool.tile([P, TILES_PER_BANK, WIDTH], F32, name="gate") for t in range(BANKS)]
+                for t in range(BANKS):
+                    nc.vector.tensor_tensor(
+                        out=gates[number][t][:].rearrange("p j (r t) -> p j r t", t=ROWS_PER_RUN),
+                        in0=units[first_round + number]["sums"][t][:].rearrange("p j (t r) -> p j r t", t=ROWS_PER_RUN),
+                        in1=bias_cols.unsqueeze(1).to_broadcast([P, TILES_PER_BANK, WIDTH // ROWS_PER_RUN, ROWS_PER_RUN]),
+                        op=ALU.add,
+                    )
+
+            number = round_at(step, SIGMOID_LAG)
+            if number is not None and number < ROUNDS_PER_GATE:
+                cols = slice(number * WIDTH, (number + 1) * WIDTH)
+                for t in range(BANKS):
+                    nc.vector.tensor_tensor(out=gates[number][t][:], in0=gates[number][t][:], in1=c_sb[:, rows_of(t), cols], op=ALU.mult)
+            if number is not None and number >= ROUNDS_PER_GATE:
+                part = number - ROUNDS_PER_GATE
+                cols = slice(part * WIDTH, (part + 1) * WIDTH)
+                for t in range(BANKS):
+                    nc.vector.tensor_tensor(out=gates[number][t][:], in0=gates[number][t][:], in1=tanhs[part][t][:], op=ALU.mult)
+                    nc.sync.dma_start(out=out_h[:, rows_of(t), cols], in_=gates[number][t][:])

@@ -22,20 +22,13 @@ SOURCES = 2
 GATES = 2
 BATCH_TILES = BATCH // P
 WIDTH = 256
-ROUNDS_PER_GATE = FEATURES // WIDTH
-ROUNDS = GATES * ROUNDS_PER_GATE
-BLOCKS = 4
+PARTS = FEATURES // WIDTH
+ROUNDS = GATES * PARTS
+HALVES = BATCH // WIDTH
+TILES = WIDTH // P
+BLOCKS = SOURCES * TILES
+SLOTS = SOURCES * PASSES
 BANK = 512
-ROWS_PER_RUN = 2
-TILES_PER_BANK = BANK // WIDTH
-BANKS = BATCH_TILES // TILES_PER_BANK
-HEAD_UNITS = 3
-SHARED_COPIES = 2
-
-MULTIPLY_LAG = 1
-SIGMOID_LAG = 2
-SUM_LAG = 3
-TANH_LAG = 4
 
 FLOPS = 2 * BATCH * (SOURCES * FEATURES) * (GATES * FEATURES)
 
@@ -48,7 +41,7 @@ def tile_lstmcell_pb_kernel(
         const = ctx.enter_context(tc.tile_pool(name="const", bufs=1))
         raw_pool = ctx.enter_context(tc.tile_pool(name="raw", bufs=1))
         grouped_pool = ctx.enter_context(tc.tile_pool(name="grouped", bufs=3))
-        act_pool = ctx.enter_context(tc.tile_pool(name="act", bufs=SOURCES))
+        act_pool = ctx.enter_context(tc.tile_pool(name="act", bufs=HALVES))
         weight_pool = ctx.enter_context(tc.tile_pool(name="weight", bufs=3))
         gate_pool = ctx.enter_context(tc.tile_pool(name="gate", bufs=10))
         cell_pool = ctx.enter_context(tc.tile_pool(name="cell", bufs=8))
@@ -57,63 +50,65 @@ def tile_lstmcell_pb_kernel(
         sums = ctx.enter_context(tc.psum_pool(name="sums", bufs=4))
         ctx.enter_context(tc.manual_schedule())
 
+        bias_rows = const.tile([P, GATES * FEATURES], BF16, name="bias_rows")
+        nc.vector.memset(bias_rows[:].bitcast(U32), 0)
         ident = const.tile([P, P], F32, name="ident")
         make_identity(nc, ident[:])
         ones = const.tile([P, P], BF16, name="ones")
         nc.vector.memset(ones[:], 1.0)
         warm = const.tile([P, 1], F32, name="warm")
         nc.vector.memset(warm[:], 0.0)
-        nc.scalar.activation(out=warm[:], in_=warm[:], func=ACT.Sigmoid)
-        bias_rows = const.tile([P, GATES * FEATURES], BF16, name="bias_rows")
-        nc.vector.memset(bias_rows[:], 0.0)
         for gate, pair in enumerate(((b_W_f, b_U_f), (b_W_o, b_U_o))):
             for row, vector in enumerate(pair):
                 nc.scalar.dma_start(
                     out=bias_rows[row : row + 1, gate * FEATURES : (gate + 1) * FEATURES],
                     in_=vector.rearrange("(o n) -> o n", o=1),
                 )
+        nc.scalar.activation(out=warm[:], in_=warm[:], func=ACT.Sigmoid)
 
         gate_weights = ((W_f, U_f), (W_o, U_o))
-        units = []
-        for name, matrix in (("x", incoming), ("h", h)):
-            by_tile = matrix.rearrange("(p b) k -> p b k", b=BATCH_TILES)
-            loads = [by_tile[:, a * ROWS_PER_RUN : (a + 1) * ROWS_PER_RUN, :] for a in range(BLOCKS // ROWS_PER_RUN)]
-            blocks = [{"slot": 0, "column": i * P} for i in range(BLOCKS)]
-            units.append({"name": name, "loads": loads, "blocks": blocks, "slots": PASSES})
+        x_rows, h_rows = (m.rearrange("(p b) k -> p b k", b=BATCH_TILES) for m in (incoming, h))
+        halves = [{"loads": [m[:, a * TILES : (a + 1) * TILES, :] for m in (x_rows, h_rows)]} for a in range(HALVES)]
+        rounds = []
         for number in range(ROUNDS):
-            gate, part = divmod(number, ROUNDS_PER_GATE)
+            gate, part = divmod(number, PARTS)
             rows = slice(part * WIDTH, (part + 1) * WIDTH)
-            loads = [gate_weights[gate][source][rows, :].rearrange("(p t) k -> p t k", t=ROWS_PER_RUN) for source in range(SOURCES)]
-            blocks = [{"slot": source * PASSES, "column": t * P} for source in range(SOURCES) for t in range(ROWS_PER_RUN)]
-            units.append({"name": "r%d" % number, "loads": loads, "blocks": blocks, "slots": SOURCES * PASSES})
-        first_round = len(units) - ROUNDS
+            view = "(t p) k -> p t k" if number == ROUNDS - 1 else "(p t) k -> p t k"
+            loads = [m[rows, :].rearrange(view, t=TILES) for m in gate_weights[gate]]
+            rounds.append({"loads": loads, "gate": gate, "part": part})
+        units = [halves[0], rounds[0], halves[1]] + rounds[1:]
 
         c_sb = raw_pool.tile([P, BATCH_TILES, FEATURES], BF16, name="c_sb")
         g_sb = raw_pool.tile([P, BATCH_TILES, FEATURES], BF16, name="g_sb")
         for index, unit in enumerate(units):
+            unit["raw"] = []
             for a, rows in enumerate(unit["loads"]):
-                raw = raw_pool.tile([P, ROWS_PER_RUN, FEATURES], BF16, name="raw_%s_%d" % (unit["name"], a))
-                nc.sync.dma_start(out=raw[:], in_=rows)
-                for t in range(ROWS_PER_RUN):
-                    unit["blocks"][a * ROWS_PER_RUN + t]["raw"] = raw[:, t, :]
-            if index == first_round + 1:
+                raw = raw_pool.tile([P, TILES, FEATURES], BF16, name="raw_%d_%d" % (index, a))
+                if index == 0 and a == 0:
+                    for t in range(TILES):
+                        nc.sync.dma_start(out=raw[:, t, :], in_=rows[:, t, :])
+                else:
+                    nc.sync.dma_start(out=raw[:], in_=rows)
+                unit["raw"] += [raw[:, t, :] for t in range(TILES)]
+            if index == 3:
                 nc.sync.dma_start(out=c_sb[:], in_=c.rearrange("(p b) n -> p b n", b=BATCH_TILES))
-            if index == first_round + 2:
+            if index == 4:
                 nc.sync.dma_start(out=g_sb[:], in_=gated_cand.rearrange("(p b) n -> p b n", b=BATCH_TILES))
 
         def transpose_unit(unit, vector_copies):
             grouped = grouped_pool.tile([P, BLOCKS * FEATURES], BF16, name="grouped", align_bytes=64)
-            grouped_words = grouped[:].bitcast(F32).rearrange("p (s r u) -> p s r u", s=unit["slots"], u=PAIRS)
-            for i, block in enumerate(unit["blocks"]):
-                raw_words = block["raw"].bitcast(F32)
+            grouped_words = grouped[:].bitcast(F32).rearrange("p (s r u) -> p s r u", s=SLOTS, u=PAIRS)
+            for i in range(BLOCKS):
+                source, t = divmod(i, TILES)
+                words = unit["raw"][i].bitcast(F32)
                 bank = transposed.tile([P, PASSES, PAIRS, P], F32, name="bank")
                 for g in range(PASSES):
                     for u in range(PAIRS):
-                        words = slice(g * K_PASS // 2 + u, (g + 1) * K_PASS // 2, PAIRS)
-                        nc.tensor.transpose(bank[:, g, u, :], raw_words[:, words], ident[:])
-                copy_out = nc.vector.tensor_copy if i >= BLOCKS - vector_copies else nc.scalar.copy
+                        picked = words[:, g * K_PASS // 2 + u : (g + 1) * K_PASS // 2 : PAIRS]
+                        nc.tensor.transpose(bank[:, g, u, :], picked, ident[:])
+                copy_out = nc.vector.tensor_copy if i in vector_copies else nc.scalar.copy
                 copy_out(
-                    out=grouped_words[:, block["slot"] : block["slot"] + PASSES, block["column"] : block["column"] + P, :],
+                    out=grouped_words[:, source * PASSES : (source + 1) * PASSES, t * P : (t + 1) * P, :],
                     in_=bank[:].rearrange("p g u r -> p g r u"),
                 )
             unit["grouped"] = grouped
@@ -125,96 +120,131 @@ def tile_lstmcell_pb_kernel(
             unit["codes"] = codes
             unit["scales"] = scales
 
-        def multiply_round(unit):
-            unit["sums"] = []
-            for t in range(BANKS):
-                bank = sums.tile([P, TILES_PER_BANK, WIDTH], F32, name="sum")
-                for j in range(TILES_PER_BANK):
-                    b = t * TILES_PER_BANK + j
-                    for slot in range(SOURCES * PASSES):
-                        source, g = divmod(slot, PASSES)
-                        m_cols = slice(g * BATCH + b * P, g * BATCH + (b + 1) * P)
-                        n_cols = slice(slot * WIDTH, (slot + 1) * WIDTH)
-                        nc.tensor.matmul_mx(
-                            out=bank[:, j, :],
-                            lhsT=units[source]["codes"][:, m_cols].bitcast(FP8X4),
-                            lhsT_scale=units[source]["scales"][:, m_cols],
-                            rhs=unit["codes"][:, n_cols].bitcast(FP8X4),
-                            rhs_scale=unit["scales"][:, n_cols],
-                            start=(slot == 0),
-                            stop=(slot == SOURCES * PASSES - 1),
-                        )
-                unit["sums"].append(bank)
-
-        def round_at(step, lag):
-            number = step - lag - first_round
-            return number if 0 <= number < ROUNDS else None
-
-        def rows_of(t):
-            return slice(t * TILES_PER_BANK, (t + 1) * TILES_PER_BANK)
-
         bias_sb = const.tile([P, GATES * FEATURES], F32, name="bias_sb")
         out_h = out_0.rearrange("(p b) n -> p b n", b=BATCH_TILES)
         out_c = out_1.rearrange("(p b) n -> p b n", b=BATCH_TILES)
-        gates = {}
-        cells = {}
-        tanhs = {}
+        tanh_of = {}
 
-        for step in range(len(units) + SIGMOID_LAG):
-            if step < len(units):
-                transpose_unit(units[step], SHARED_COPIES if step < HEAD_UNITS else 0)
-            for q in range(GATES * FEATURES // BANK):
-                if step == 1 + q // (FEATURES // BANK):
-                    bank = sums.tile([P, BANK], F32, name="sum")
-                    nc.tensor.matmul(out=bank[:], lhsT=ones[:], rhs=bias_rows[:, q * BANK : (q + 1) * BANK], start=True, stop=True)
-                    nc.scalar.copy(out=bias_sb[:, q * BANK : (q + 1) * BANK], in_=bank[:])
+        def piece(number, half, tiles=(0, TILES), cols=(0, WIDTH)):
+            part = rounds[number]["part"]
+            return {
+                "number": number,
+                "half": half,
+                "tiles": range(*tiles),
+                "cols": slice(*cols),
+                "width": cols[1] - cols[0],
+                "rows": slice(half * TILES + tiles[0], half * TILES + tiles[1]),
+                "out": slice(part * WIDTH + cols[0], part * WIDTH + cols[1]),
+                "shape": [P, tiles[1] - tiles[0], cols[1] - cols[0]],
+            }
 
-            number = round_at(step, SIGMOID_LAG)
-            if number is not None:
-                for t in range(BANKS):
-                    nc.scalar.activation(out=gates[number][t][:], in_=gates[number][t][:], func=ACT.Sigmoid)
-
-            number = round_at(step, TANH_LAG)
-            if number is not None and number < ROUNDS_PER_GATE:
-                cols = slice(number * WIDTH, (number + 1) * WIDTH)
-                tanhs[number] = [tanh_pool.tile([P, TILES_PER_BANK, WIDTH], F32, name="tanh_c") for t in range(BANKS)]
-                for t in range(BANKS):
-                    nc.scalar.activation(out=tanhs[number][t][:], in_=cells[number][t][:], func=ACT.Tanh)
-                    nc.sync.dma_start(out=out_c[:, rows_of(t), cols], in_=cells[number][t][:])
-
-            number = round_at(step, SUM_LAG)
-            if number is not None and number < ROUNDS_PER_GATE:
-                cols = slice(number * WIDTH, (number + 1) * WIDTH)
-                cells[number] = [cell_pool.tile([P, TILES_PER_BANK, WIDTH], F32, name="cell") for t in range(BANKS)]
-                for t in range(BANKS):
-                    nc.vector.tensor_tensor(out=cells[number][t][:], in0=gates[number][t][:], in1=g_sb[:, rows_of(t), cols], op=ALU.add)
-
-            number = round_at(step, MULTIPLY_LAG)
-            if number is not None:
-                multiply_round(units[first_round + number])
-
-            if step < len(units):
-                quantise_unit(units[step], act_pool if step < first_round else weight_pool)
-
-            if number is not None:
-                bias_cols = bias_sb[:, number * WIDTH : (number + 1) * WIDTH].rearrange("p (r t) -> p r t", t=ROWS_PER_RUN)
-                gates[number] = [gate_pool.tile([P, TILES_PER_BANK, WIDTH], F32, name="gate") for t in range(BANKS)]
-                for t in range(BANKS):
-                    nc.vector.tensor_tensor(
-                        out=gates[number][t][:].rearrange("p j (r t) -> p j r t", t=ROWS_PER_RUN),
-                        in0=units[first_round + number]["sums"][t][:].rearrange("p j (t r) -> p j r t", t=ROWS_PER_RUN),
-                        in1=bias_cols.unsqueeze(1).to_broadcast([P, TILES_PER_BANK, WIDTH // ROWS_PER_RUN, ROWS_PER_RUN]),
-                        op=ALU.add,
+        def multiply(item):
+            unit = rounds[item["number"]]
+            acts = halves[item["half"]]
+            bank = sums.tile(item["shape"], F32, name="sum")
+            for index, j in enumerate(item["tiles"]):
+                for slot in range(SLOTS):
+                    m_cols = slice(slot * WIDTH + j * P, slot * WIDTH + (j + 1) * P)
+                    n_cols = slice(slot * WIDTH + item["cols"].start, slot * WIDTH + item["cols"].stop)
+                    nc.tensor.matmul_mx(
+                        out=bank[:, index, :],
+                        lhsT=acts["codes"][:, m_cols].bitcast(FP8X4),
+                        lhsT_scale=acts["scales"][:, m_cols],
+                        rhs=unit["codes"][:, n_cols].bitcast(FP8X4),
+                        rhs_scale=unit["scales"][:, n_cols],
+                        start=(slot == 0),
+                        stop=(slot == SLOTS - 1),
                     )
+            item["sums"] = bank
 
-            number = round_at(step, SIGMOID_LAG)
-            if number is not None and number < ROUNDS_PER_GATE:
-                cols = slice(number * WIDTH, (number + 1) * WIDTH)
-                for t in range(BANKS):
-                    nc.vector.tensor_tensor(out=gates[number][t][:], in0=gates[number][t][:], in1=c_sb[:, rows_of(t), cols], op=ALU.mult)
-            if number is not None and number >= ROUNDS_PER_GATE:
-                part = number - ROUNDS_PER_GATE
-                cols = slice(part * WIDTH, (part + 1) * WIDTH)
-                for t in range(BANKS):
-                    nc.vector.tensor_tensor(out=gates[number][t][:], in0=gates[number][t][:], in1=tanhs[part][t][:], op=ALU.mult)
-                    nc.sync.dma_start(out=out_h[:, rows_of(t), cols], in_=gates[number][t][:])
+        def add_bias(item):
+            unit = rounds[item["number"]]
+            first = unit["gate"] * FEATURES
+            bias_cols = bias_sb[:, first + item["out"].start : first + item["out"].stop]
+            gate = gate_pool.tile(item["shape"], F32, name="gate")
+            out = gate[:]
+            in0 = item["sums"][:]
+            in1 = bias_cols.unsqueeze(1).to_broadcast(item["shape"])
+            if item["number"] < ROUNDS - 1:
+                out = out.rearrange("p j (r t) -> p j r t", t=TILES)
+                in0 = in0.rearrange("p j (t r) -> p j r t", t=TILES)
+                in1 = bias_cols.rearrange("p (r t) -> p r t", t=TILES).unsqueeze(1).to_broadcast([P, len(item["tiles"]), WIDTH // TILES, TILES])
+            nc.vector.tensor_tensor(out=out, in0=in0, in1=in1, op=ALU.add)
+            item["gate"] = gate
+
+        def sigmoid(item):
+            nc.scalar.activation(out=item["gate"][:], in_=item["gate"][:], func=ACT.Sigmoid)
+
+        def times_c(item):
+            gate = item["gate"]
+            nc.vector.tensor_tensor(out=gate[:], in0=gate[:], in1=c_sb[:, item["rows"], item["out"]], op=ALU.mult)
+
+        def plus_g(item, engine):
+            cell = cell_pool.tile(item["shape"], F32, name="cell")
+            engine.tensor_tensor(out=cell[:], in0=item["gate"][:], in1=g_sb[:, item["rows"], item["out"]], op=ALU.add)
+            item["cell"] = cell
+            nc.sync.dma_start(out=out_c[:, item["rows"], item["out"]], in_=cell[:])
+
+        def tanh(item):
+            tile = tanh_pool.tile(item["shape"], F32, name="tanh_c")
+            nc.scalar.activation(out=tile[:], in_=item["cell"][:], func=ACT.Tanh)
+            tanh_of[rounds[item["number"]]["part"], item["half"]] = tile
+
+        def times_tanh(item, engine):
+            gate = item["gate"]
+            factor = tanh_of[rounds[item["number"]]["part"], item["half"]]
+            engine.tensor_tensor(out=gate[:], in0=gate[:], in1=factor[:, item["tiles"].start : item["tiles"].stop, item["cols"]], op=ALU.mult)
+            nc.sync.dma_start(out=out_h[:, item["rows"], item["out"]], in_=gate[:])
+
+        for q in range(GATES * FEATURES // BANK):
+            bank = sums.tile([P, BANK], F32, name="sum")
+            nc.tensor.matmul(out=bank[:], lhsT=ones[:], rhs=bias_rows[:, q * BANK : (q + 1) * BANK], start=True, stop=True)
+            nc.scalar.copy(out=bias_sb[:, q * BANK : (q + 1) * BANK], in_=bank[:])
+
+        vector_blocks = [[3],[3],[],[],[],[],[],[],[],[2,3]]
+        lag = 1
+        last_step = ROUNDS + 1 + lag
+        when = {}
+        for number in range(ROUNDS):
+            step = number + 2 + lag if number else None
+            halves_at = (step, step) if number else (2,3)
+            for half in range(HALVES):
+                if number == ROUNDS - 1 and half == HALVES - 1:
+                    when[step] += [piece(number, half, tiles=(0, 1)), piece(number, half, tiles=(1, 2), cols=(0, P)), piece(number, half, tiles=(1, 2), cols=(P, WIDTH))]
+                else:
+                    when.setdefault(halves_at[half], []).append(piece(number, half))
+        def of_gate(step, gate):
+            return [item for item in when.get(step, []) if rounds[item["number"]]["gate"] == gate]
+        for step in range(last_step):
+            items = when.get(step, [])
+            if step < len(units):
+                transpose_unit(units[step], vector_blocks[step])
+            for item in when.get(step - 1, []):
+                sigmoid(item)
+            for item in of_gate(step - 2, 0):
+                tanh(item)
+            for item in items:
+                multiply(item)
+            if step < len(units):
+                quantise_unit(units[step], act_pool if step in (0, 2) else weight_pool)
+            for item in of_gate(step - 1, 0):
+                times_c(item)
+            for item in items:
+                add_bias(item)
+            for item in of_gate(step - 1, 0):
+                plus_g(item, nc.vector)
+            for item in of_gate(step - 1, 1):
+                times_tanh(item, nc.vector)
+        for item in when[last_step - 1]:
+            sigmoid(item)
+        for item in when[last_step]:
+            multiply(item)
+        done = of_gate(last_step - 1, 1)
+        for index, item in enumerate(when[last_step]):
+            add_bias(item)
+            sigmoid(item)
+            if index < len(done):
+                times_tanh(done[index], nc.vector)
+            if index:
+                times_tanh(when[last_step][index - 1], nc.vector)
+        times_tanh(when[last_step][-1], nc.vector)

@@ -196,11 +196,6 @@ def tile_lstmcell_pb_kernel(
             engine.tensor_tensor(out=gate[:], in0=gate[:], in1=factor[:, item["tiles"].start : item["tiles"].stop, item["cols"]], op=ALU.mult)
             nc.sync.dma_start(out=out_h[:, item["rows"], item["out"]], in_=gate[:])
 
-        for q in range(GATES * FEATURES // BANK):
-            bank = sums.tile([P, BANK], F32, name="sum")
-            nc.tensor.matmul(out=bank[:], lhsT=ones[:], rhs=bias_rows[:, q * BANK : (q + 1) * BANK], start=True, stop=True)
-            nc.scalar.copy(out=bias_sb[:, q * BANK : (q + 1) * BANK], in_=bank[:])
-
         vector_blocks = [[3],[3],[],[],[],[],[],[],[],[2,3]]
         lag = 1
         last_step = ROUNDS + 1 + lag
@@ -219,6 +214,11 @@ def tile_lstmcell_pb_kernel(
             items = when.get(step, [])
             if step < len(units):
                 transpose_unit(units[step], vector_blocks[step])
+            for q in range(GATES * FEATURES // BANK):
+                if step == 1 + q // (FEATURES // BANK):
+                    bank = sums.tile([P, BANK], F32, name="sum")
+                    nc.tensor.matmul(out=bank[:], lhsT=ones[:], rhs=bias_rows[:, q * BANK : (q + 1) * BANK], start=True, stop=True)
+                    nc.scalar.copy(out=bias_sb[:, q * BANK : (q + 1) * BANK], in_=bank[:])
             for item in when.get(step - 1, []):
                 sigmoid(item)
             for item in of_gate(step - 2, 0):

@@ -29,6 +29,8 @@ TILES = WIDTH // P
 BLOCKS = SOURCES * TILES
 SLOTS = SOURCES * PASSES
 BANK = 512
+TURNED = 2
+FIRST_TURNED = ROUNDS - TURNED
 
 FLOPS = 2 * BATCH * (SOURCES * FEATURES) * (GATES * FEATURES)
 
@@ -43,9 +45,11 @@ def tile_lstmcell_pb_kernel(
         grouped_pool = ctx.enter_context(tc.tile_pool(name="grouped", bufs=3))
         act_pool = ctx.enter_context(tc.tile_pool(name="act", bufs=HALVES))
         weight_pool = ctx.enter_context(tc.tile_pool(name="weight", bufs=3))
-        gate_pool = ctx.enter_context(tc.tile_pool(name="gate", bufs=10))
-        cell_pool = ctx.enter_context(tc.tile_pool(name="cell", bufs=8))
-        tanh_pool = ctx.enter_context(tc.tile_pool(name="tanh", bufs=8))
+        gate_pool = ctx.enter_context(tc.tile_pool(name="gate", bufs=4))
+        turned_pool = ctx.enter_context(tc.tile_pool(name="turned", bufs=4))
+        half_pool = ctx.enter_context(tc.tile_pool(name="half", bufs=6))
+        cell_pool = ctx.enter_context(tc.tile_pool(name="cell", bufs=4))
+        tanh_pool = ctx.enter_context(tc.tile_pool(name="tanh", bufs=4))
         transposed = ctx.enter_context(tc.psum_pool(name="transposed", bufs=4))
         sums = ctx.enter_context(tc.psum_pool(name="sums", bufs=4))
         ctx.enter_context(tc.manual_schedule())
@@ -104,7 +108,7 @@ def tile_lstmcell_pb_kernel(
                 bank = transposed.tile([P, PASSES, PAIRS, P], F32, name="bank")
                 for g in range(PASSES):
                     for u in range(PAIRS):
-                        picked = words[:, g * K_PASS // 2 + u : (g + 1) * K_PASS // 2 : PAIRS]
+                        picked = words[:, g * K_PASS // PAIRS + u : (g + 1) * K_PASS // PAIRS : PAIRS]
                         nc.tensor.transpose(bank[:, g, u, :], picked, ident[:])
                 copy_out = nc.vector.tensor_copy if i in vector_copies else nc.scalar.copy
                 copy_out(
@@ -120,131 +124,183 @@ def tile_lstmcell_pb_kernel(
             unit["codes"] = codes
             unit["scales"] = scales
 
-        bias_sb = const.tile([P, GATES * FEATURES], F32, name="bias_sb")
+        def product(out, stationary, s_first, moving, m_first, m_width):
+            for slot in range(SLOTS):
+                s_cols = slice(slot * WIDTH + s_first, slot * WIDTH + s_first + P)
+                m_cols = slice(slot * WIDTH + m_first, slot * WIDTH + m_first + m_width)
+                nc.tensor.matmul_mx(
+                    out=out,
+                    lhsT=stationary["codes"][:, s_cols].bitcast(FP8X4),
+                    lhsT_scale=stationary["scales"][:, s_cols],
+                    rhs=moving["codes"][:, m_cols].bitcast(FP8X4),
+                    rhs_scale=moving["scales"][:, m_cols],
+                    start=(slot == 0),
+                    stop=(slot == SLOTS - 1),
+                )
+
+        bias_sb = const.tile([P, FIRST_TURNED * WIDTH], F32, name="bias_sb")
+        bias_turned = const.tile([P, TURNED * TILES], F32, name="bias_turned")
         out_h = out_0.rearrange("(p b) n -> p b n", b=BATCH_TILES)
         out_c = out_1.rearrange("(p b) n -> p b n", b=BATCH_TILES)
-        tanh_of = {}
 
-        def piece(number, half, tiles=(0, TILES), cols=(0, WIDTH)):
+        def columns(number):
             part = rounds[number]["part"]
-            return {
-                "number": number,
-                "half": half,
-                "tiles": range(*tiles),
-                "cols": slice(*cols),
-                "width": cols[1] - cols[0],
-                "rows": slice(half * TILES + tiles[0], half * TILES + tiles[1]),
-                "out": slice(part * WIDTH + cols[0], part * WIDTH + cols[1]),
-                "shape": [P, tiles[1] - tiles[0], cols[1] - cols[0]],
-            }
+            return slice(part * WIDTH, (part + 1) * WIDTH)
 
-        def multiply(item):
-            unit = rounds[item["number"]]
-            acts = halves[item["half"]]
-            bank = sums.tile(item["shape"], F32, name="sum")
-            for index, j in enumerate(item["tiles"]):
-                for slot in range(SLOTS):
-                    m_cols = slice(slot * WIDTH + j * P, slot * WIDTH + (j + 1) * P)
-                    n_cols = slice(slot * WIDTH + item["cols"].start, slot * WIDTH + item["cols"].stop)
-                    nc.tensor.matmul_mx(
-                        out=bank[:, index, :],
-                        lhsT=acts["codes"][:, m_cols].bitcast(FP8X4),
-                        lhsT_scale=acts["scales"][:, m_cols],
-                        rhs=unit["codes"][:, n_cols].bitcast(FP8X4),
-                        rhs_scale=unit["scales"][:, n_cols],
-                        start=(slot == 0),
-                        stop=(slot == SLOTS - 1),
-                    )
-            item["sums"] = bank
+        def multiply(number, half):
+            bank = sums.tile([P, TILES, WIDTH], F32, name="sum")
+            for j in range(TILES):
+                product(bank[:, j, :], halves[half], j * P, rounds[number], 0, WIDTH)
+            rounds[number].setdefault("sums", {})[half] = bank
 
-        def add_bias(item):
-            unit = rounds[item["number"]]
-            first = unit["gate"] * FEATURES
-            bias_cols = bias_sb[:, first + item["out"].start : first + item["out"].stop]
-            gate = gate_pool.tile(item["shape"], F32, name="gate")
-            out = gate[:]
-            in0 = item["sums"][:]
-            in1 = bias_cols.unsqueeze(1).to_broadcast(item["shape"])
-            if item["number"] < ROUNDS - 1:
+        def add_bias(number, half):
+            unit = rounds[number]
+            if half == 0:
+                unit["gate_tile"] = gate_pool.tile([P, BATCH_TILES, WIDTH], F32, name="gate")
+            bias = bias_sb[:, number * WIDTH : (number + 1) * WIDTH].rearrange("p (r t) -> p r t", t=TILES)
+            nc.vector.tensor_tensor(
+                out=unit["gate_tile"][:, half * TILES : (half + 1) * TILES, :].rearrange("p j (r t) -> p j r t", t=TILES),
+                in0=unit["sums"][half][:].rearrange("p j (t r) -> p j r t", t=TILES),
+                in1=bias.unsqueeze(1).to_broadcast([P, TILES, WIDTH // TILES, TILES]),
+                op=ALU.add,
+            )
+
+        def sigmoid(number):
+            gate = rounds[number]["gate_tile"]
+            nc.scalar.activation(out=gate[:], in_=gate[:], func=ACT.Sigmoid)
+
+        def times_c(number):
+            gate = rounds[number]["gate_tile"]
+            nc.vector.tensor_tensor(out=gate[:], in0=gate[:], in1=c_sb[:, :, columns(number)], op=ALU.mult)
+
+        def plus_g(number):
+            cell = cell_pool.tile([P, BATCH_TILES, WIDTH], F32, name="cell")
+            nc.vector.tensor_tensor(out=cell[:], in0=rounds[number]["gate_tile"][:], in1=g_sb[:, :, columns(number)], op=ALU.add)
+            nc.sync.dma_start(out=out_c[:, :, columns(number)], in_=cell[:])
+            rounds[number]["cell"] = cell
+
+        def tanh(number):
+            tile = tanh_pool.tile([P, BATCH_TILES, WIDTH], F32, name="tanh_c")
+            nc.scalar.activation(out=tile[:], in_=rounds[number]["cell"][:], func=ACT.Tanh)
+            rounds[number + PARTS]["tanh"] = tile
+
+        def times_tanh(number):
+            unit = rounds[number]
+            gate = unit["gate_tile"]
+            nc.vector.tensor_tensor(out=gate[:], in0=gate[:], in1=unit["tanh"][:], op=ALU.mult)
+            nc.sync.dma_start(out=out_h[:, :, columns(number)], in_=gate[:])
+
+        def multiply_turned(number, t, half):
+            unit = rounds[number]
+            bank = sums.tile([P, WIDTH], F32, name="sum")
+            product(bank[:], unit, t * P, halves[half], 0, WIDTH)
+            unit.setdefault("sums", {})[t, half] = bank
+
+        def sigmoid_turned(number, t, half):
+            unit = rounds[number]
+            index = (number - FIRST_TURNED) * TILES + t
+            tile = turned_pool.tile([P, WIDTH], F32, name="gate_t")
+            nc.scalar.activation(out=tile[:], in_=unit["sums"][t, half][:], func=ACT.Sigmoid, bias=bias_turned[:, index : index + 1])
+            unit.setdefault("gate_t", {})[t, half] = tile
+
+        def turn(number, t, half):
+            unit = rounds[number]
+            together = number < ROUNDS - 1
+            if t == 0 or not together:
+                unit.setdefault("turned", {})[t, half] = transposed.tile([P, TILES, TILES if together else 1, P], F32, name="bank")
+            bank = unit["turned"][0 if together else t, half]
+            for j in range(TILES):
+                nc.tensor.transpose(bank[:, j, t if together else 0, :], unit["gate_t"][t, half][:, j * P : (j + 1) * P], ident[:])
+
+        def finish(number, half, t=None):
+            unit = rounds[number]
+            rows = slice(half * TILES, (half + 1) * TILES)
+            bank = unit["turned"][0 if t is None else t, half]
+            if t is None:
+                cols = slice(0, WIDTH)
+                in0 = bank[:].rearrange("p j t r -> p j r t")
+            else:
+                cols = slice(t * P, (t + 1) * P)
+                in0 = bank[:, :, 0, :]
+            tile = half_pool.tile([P, TILES, WIDTH if t is None else P], F32, name="hidden")
+            out = tile[:]
+            in1 = unit["tanh"][:, rows, cols]
+            if t is None:
                 out = out.rearrange("p j (r t) -> p j r t", t=TILES)
-                in0 = in0.rearrange("p j (t r) -> p j r t", t=TILES)
-                in1 = bias_cols.rearrange("p (r t) -> p r t", t=TILES).unsqueeze(1).to_broadcast([P, len(item["tiles"]), WIDTH // TILES, TILES])
-            nc.vector.tensor_tensor(out=out, in0=in0, in1=in1, op=ALU.add)
-            item["gate"] = gate
+                in1 = in1.rearrange("p j (r t) -> p j r t", t=TILES)
+            nc.vector.tensor_tensor(out=out, in0=in0, in1=in1, op=ALU.mult)
+            first = unit["part"] * WIDTH
+            nc.sync.dma_start(out=out_h[:, rows, first + cols.start : first + cols.stop], in_=tile[:])
 
-        def sigmoid(item):
-            nc.scalar.activation(out=item["gate"][:], in_=item["gate"][:], func=ACT.Sigmoid)
-
-        def times_c(item):
-            gate = item["gate"]
-            nc.vector.tensor_tensor(out=gate[:], in0=gate[:], in1=c_sb[:, item["rows"], item["out"]], op=ALU.mult)
-
-        def plus_g(item, engine):
-            cell = cell_pool.tile(item["shape"], F32, name="cell")
-            engine.tensor_tensor(out=cell[:], in0=item["gate"][:], in1=g_sb[:, item["rows"], item["out"]], op=ALU.add)
-            item["cell"] = cell
-            nc.sync.dma_start(out=out_c[:, item["rows"], item["out"]], in_=cell[:])
-
-        def tanh(item):
-            tile = tanh_pool.tile(item["shape"], F32, name="tanh_c")
-            nc.scalar.activation(out=tile[:], in_=item["cell"][:], func=ACT.Tanh)
-            tanh_of[rounds[item["number"]]["part"], item["half"]] = tile
-
-        def times_tanh(item, engine):
-            gate = item["gate"]
-            factor = tanh_of[rounds[item["number"]]["part"], item["half"]]
-            engine.tensor_tensor(out=gate[:], in0=gate[:], in1=factor[:, item["tiles"].start : item["tiles"].stop, item["cols"]], op=ALU.mult)
-            nc.sync.dma_start(out=out_h[:, item["rows"], item["out"]], in_=gate[:])
-
-        vector_blocks = [[3],[3],[],[],[],[],[],[],[],[2,3]]
-        lag = 1
-        last_step = ROUNDS + 1 + lag
-        when = {}
-        for number in range(ROUNDS):
-            step = number + 2 + lag if number else None
-            halves_at = (step, step) if number else (2,3)
-            for half in range(HALVES):
-                if number == ROUNDS - 1 and half == HALVES - 1:
-                    when[step] += [piece(number, half, tiles=(0, 1)), piece(number, half, tiles=(1, 2), cols=(0, P)), piece(number, half, tiles=(1, 2), cols=(P, WIDTH))]
-                else:
-                    when.setdefault(halves_at[half], []).append(piece(number, half))
-        def of_gate(step, gate):
-            return [item for item in when.get(step, []) if rounds[item["number"]]["gate"] == gate]
-        for step in range(last_step):
-            items = when.get(step, [])
+        vector_blocks = [[3],[3],[],[],[],[],[],[],[],[]]
+        for step in range(ROUNDS + 2):
+            number = step - 3
+            before = number - 1
             if step < len(units):
                 transpose_unit(units[step], vector_blocks[step])
-            for q in range(GATES * FEATURES // BANK):
-                if step == 1 + q // (FEATURES // BANK):
+            if step == 1:
+                for first in range(0, FIRST_TURNED * WIDTH, BANK):
                     bank = sums.tile([P, BANK], F32, name="sum")
-                    nc.tensor.matmul(out=bank[:], lhsT=ones[:], rhs=bias_rows[:, q * BANK : (q + 1) * BANK], start=True, stop=True)
-                    nc.scalar.copy(out=bias_sb[:, q * BANK : (q + 1) * BANK], in_=bank[:])
-            for item in when.get(step - 1, []):
-                sigmoid(item)
-            for item in of_gate(step - 2, 0):
-                tanh(item)
-            for item in items:
-                multiply(item)
+                    nc.tensor.matmul(out=bank[:], lhsT=ones[:], rhs=bias_rows[:, first : first + BANK], start=True, stop=True)
+                    nc.scalar.copy(out=bias_sb[:, first : first + BANK], in_=bank[:])
+            if step == 2:
+                bank = sums.tile([P, TURNED * TILES], F32, name="sum")
+                for index in range(TURNED * TILES):
+                    n, t = divmod(index, TILES)
+                    first = (FIRST_TURNED + n) * WIDTH
+                    cols = slice(first + t * P, first + (t + 1) * P) if FIRST_TURNED + n == ROUNDS - 1 else slice(first + t, first + WIDTH, TILES)
+                    nc.tensor.matmul(out=bank[:, index : index + 1], lhsT=bias_rows[:, cols], rhs=ones[:, 0:1], start=True, stop=True)
+                nc.scalar.copy(out=bias_turned[:], in_=bank[:])
+            if 0 <= before < FIRST_TURNED:
+                sigmoid(before)
+            if 0 <= before - 1 < PARTS:
+                tanh(before - 1)
+            if step == 2:
+                multiply(0, 0)
+            if step == 3:
+                multiply(0, 1)
+            elif 1 <= number < FIRST_TURNED:
+                for half in range(HALVES):
+                    multiply(number, half)
+            elif number >= FIRST_TURNED and number < ROUNDS - 1:
+                for t in range(TILES):
+                    for half in range(HALVES):
+                        multiply_turned(number, t, half)
+                for t in range(TILES):
+                    for half in range(HALVES):
+                        sigmoid_turned(number, t, half)
+
             if step < len(units):
                 quantise_unit(units[step], act_pool if step in (0, 2) else weight_pool)
-            for item in of_gate(step - 1, 0):
-                times_c(item)
-            for item in items:
-                add_bias(item)
-            for item in of_gate(step - 1, 0):
-                plus_g(item, nc.vector)
-            for item in of_gate(step - 1, 1):
-                times_tanh(item, nc.vector)
-        for item in when[last_step - 1]:
-            sigmoid(item)
-        for item in when[last_step]:
-            multiply(item)
-        done = of_gate(last_step - 1, 1)
-        for index, item in enumerate(when[last_step]):
-            add_bias(item)
-            sigmoid(item)
-            if index < len(done):
-                times_tanh(done[index], nc.vector)
-            if index:
-                times_tanh(when[last_step][index - 1], nc.vector)
-        times_tanh(when[last_step][-1], nc.vector)
+            if 0 <= before < PARTS:
+                times_c(before)
+            if step == 2:
+                add_bias(0, 0)
+            if step == 3:
+                add_bias(0, 1)
+            elif 1 <= number < FIRST_TURNED:
+                for half in range(HALVES):
+                    add_bias(number, half)
+            if 0 <= before < PARTS:
+                plus_g(before)
+            if PARTS <= before < FIRST_TURNED:
+                times_tanh(before)
+
+        last = ROUNDS - 1
+        before = last - 1
+        for half in range(HALVES):
+            multiply_turned(last, 0, half)
+        for half in range(HALVES):
+            for t in range(TILES):
+                turn(before, t, half)
+        multiply_turned(last, 1, 0)
+        multiply_turned(last, 1, 1)
+        for t in range(TILES):
+            for half in range(HALVES):
+                sigmoid_turned(last, t, half)
+        for half in range(HALVES):
+            finish(before, half)
+        for t in range(TILES):
+            for half in range(HALVES):
+                turn(last, t, half)
+                finish(last, half, t)

@@ -94,9 +94,9 @@ def tile_lstmcell_pb_kernel(
                 else:
                     nc.sync.dma_start(out=raw[:], in_=rows)
                 unit["raw"] += [raw[:, t, :] for t in range(TILES)]
-            if index == 3:
-                nc.sync.dma_start(out=c_sb[:], in_=c.rearrange("(p b) n -> p b n", b=BATCH_TILES))
             if index == 4:
+                nc.sync.dma_start(out=c_sb[:], in_=c.rearrange("(p b) n -> p b n", b=BATCH_TILES))
+            if index == 5:
                 nc.sync.dma_start(out=g_sb[:], in_=gated_cand.rearrange("(p b) n -> p b n", b=BATCH_TILES))
 
         def transpose_unit(unit, vector_copies):

@@ -62,12 +62,6 @@ def tile_lstmcell_pb_kernel(
         nc.vector.memset(ones[:], 1.0)
         warm = const.tile([P, 1], F32, name="warm")
         nc.vector.memset(warm[:], 0.0)
-        for gate, pair in enumerate(((b_W_f, b_U_f), (b_W_o, b_U_o))):
-            for row, vector in enumerate(pair):
-                nc.scalar.dma_start(
-                    out=bias_rows[row : row + 1, gate * FEATURES : (gate + 1) * FEATURES],
-                    in_=vector.rearrange("(o n) -> o n", o=1),
-                )
         nc.scalar.activation(out=warm[:], in_=warm[:], func=ACT.Sigmoid)
 
         gate_weights = ((W_f, U_f), (W_o, U_o))
@@ -94,6 +88,13 @@ def tile_lstmcell_pb_kernel(
                 else:
                     nc.sync.dma_start(out=raw[:], in_=rows)
                 unit["raw"] += [raw[:, t, :] for t in range(TILES)]
+            if index == 1:
+                for gate, pair in enumerate(((b_W_f, b_U_f), (b_W_o, b_U_o))):
+                    for row, vector in enumerate(pair):
+                        nc.scalar.dma_start(
+                            out=bias_rows[row : row + 1, gate * FEATURES : (gate + 1) * FEATURES],
+                            in_=vector.rearrange("(o n) -> o n", o=1),
+                        )
             if index == 4:
                 nc.sync.dma_start(out=c_sb[:], in_=c.rearrange("(p b) n -> p b n", b=BATCH_TILES))
             if index == 5:

@@ -28,7 +28,12 @@ HALVES = BATCH // WIDTH
 TILES = WIDTH // P
 BLOCKS = SOURCES * TILES
 SLOTS = SOURCES * PASSES
+HEAD_UNITS = 2
+BIAS_UNIT = 1
+C_UNIT = 5
+G_UNIT = 5
 BANK = 512
+ORDERED_UNITS = (4, 5)
 TURNED = 2
 FIRST_TURNED = ROUNDS - TURNED
 
@@ -42,6 +47,7 @@ def tile_lstmcell_pb_kernel(
     with ExitStack() as ctx:
         const = ctx.enter_context(tc.tile_pool(name="const", bufs=1))
         raw_pool = ctx.enter_context(tc.tile_pool(name="raw", bufs=1))
+        ordered_pool = ctx.enter_context(tc.tile_pool(name="ordered", bufs=4))
         grouped_pool = ctx.enter_context(tc.tile_pool(name="grouped", bufs=3))
         act_pool = ctx.enter_context(tc.tile_pool(name="act", bufs=HALVES))
         weight_pool = ctx.enter_context(tc.tile_pool(name="weight", bufs=3))
@@ -76,10 +82,14 @@ def tile_lstmcell_pb_kernel(
             rounds.append({"loads": loads, "gate": gate, "part": part})
         units = [halves[0], rounds[0], halves[1]] + rounds[1:]
 
+        for unit in units:
+            unit["by_tile"] = unit is units[-1]
+
         c_sb = raw_pool.tile([P, BATCH_TILES, FEATURES], BF16, name="c_sb")
         g_sb = raw_pool.tile([P, BATCH_TILES, FEATURES], BF16, name="g_sb")
         for index, unit in enumerate(units):
             unit["raw"] = []
+            unit["rows"] = []
             for a, rows in enumerate(unit["loads"]):
                 raw = raw_pool.tile([P, TILES, FEATURES], BF16, name="raw_%d_%d" % (index, a))
                 if index == 0 and a == 0:
@@ -87,33 +97,58 @@ def tile_lstmcell_pb_kernel(
                         nc.sync.dma_start(out=raw[:, t, :], in_=rows[:, t, :])
                 else:
                     nc.sync.dma_start(out=raw[:], in_=rows)
+                unit["rows"].append(raw)
                 unit["raw"] += [raw[:, t, :] for t in range(TILES)]
-            if index == 1:
+            if index == BIAS_UNIT:
                 for gate, pair in enumerate(((b_W_f, b_U_f), (b_W_o, b_U_o))):
                     for row, vector in enumerate(pair):
                         nc.scalar.dma_start(
                             out=bias_rows[row : row + 1, gate * FEATURES : (gate + 1) * FEATURES],
                             in_=vector.rearrange("(o n) -> o n", o=1),
                         )
-            if index == 4:
+            if index == C_UNIT:
                 nc.sync.dma_start(out=c_sb[:], in_=c.rearrange("(p b) n -> p b n", b=BATCH_TILES))
-            if index == 5:
+            if index == G_UNIT:
                 nc.sync.dma_start(out=g_sb[:], in_=gated_cand.rearrange("(p b) n -> p b n", b=BATCH_TILES))
 
-        def transpose_unit(unit, vector_copies):
+        def order_words(unit):
+            unit["ordered"] = []
+            for raw in unit["rows"]:
+                ordered = ordered_pool.tile([P, TILES, FEATURES], BF16, name="ordered")
+                nc.vector.tensor_copy(
+                    out=ordered[:].bitcast(F32).rearrange("p t (u w) -> p t u w", u=PAIRS),
+                    in_=raw[:].bitcast(F32).rearrange("p t (w u) -> p t u w", u=PAIRS),
+                )
+                unit["ordered"] += [ordered[:, t, :] for t in range(TILES)]
+
+        def transpose_unit(unit, vector_block):
             grouped = grouped_pool.tile([P, BLOCKS * FEATURES], BF16, name="grouped", align_bytes=64)
             grouped_words = grouped[:].bitcast(F32).rearrange("p (s r u) -> p s r u", s=SLOTS, u=PAIRS)
-            for i in range(BLOCKS):
-                source, t = divmod(i, TILES)
-                words = unit["raw"][i].bitcast(F32)
+            if unit["by_tile"]:
+                grouped_tiles = grouped[:].bitcast(F32).rearrange("p (t s r u) -> p t s r u", t=TILES, s=SLOTS, u=PAIRS)
+            for n in range(BLOCKS):
+                if unit["by_tile"]:
+                    t, source = divmod(n, SOURCES)
+                else:
+                    source, t = divmod(n, TILES)
+                i = source * TILES + t
+                in_order = "ordered" in unit
+                words = unit["ordered" if in_order else "raw"][i].bitcast(F32)
                 bank = transposed.tile([P, PASSES, PAIRS, P], F32, name="bank")
                 for g in range(PASSES):
                     for u in range(PAIRS):
-                        picked = words[:, g * K_PASS // PAIRS + u : (g + 1) * K_PASS // PAIRS : PAIRS]
+                        if in_order:
+                            picked = words[:, (u * PASSES + g) * P : (u * PASSES + g + 1) * P]
+                        else:
+                            picked = words[:, g * K_PASS // PAIRS + u : (g + 1) * K_PASS // PAIRS : PAIRS]
                         nc.tensor.transpose(bank[:, g, u, :], picked, ident[:])
-                copy_out = nc.vector.tensor_copy if i in vector_copies else nc.scalar.copy
+                copy_out = nc.vector.tensor_copy if n == vector_block else nc.scalar.copy
+                if unit["by_tile"]:
+                    words_out = grouped_tiles[:, t, source * PASSES : (source + 1) * PASSES, :, :]
+                else:
+                    words_out = grouped_words[:, source * PASSES : (source + 1) * PASSES, t * P : (t + 1) * P, :]
                 copy_out(
-                    out=grouped_words[:, source * PASSES : (source + 1) * PASSES, t * P : (t + 1) * P, :],
+                    out=words_out,
                     in_=bank[:].rearrange("p g u r -> p g r u"),
                 )
             unit["grouped"] = grouped
@@ -121,13 +156,22 @@ def tile_lstmcell_pb_kernel(
         def quantise_unit(unit, pool):
             codes = pool.tile([P, BLOCKS * FEATURES // PACK], U32, name="codes", align_bytes=64)
             scales = pool.tile([P, BLOCKS * FEATURES // PACK], U8, name="scales", align_bytes=64)
-            nc.vector.quantize_mx(out=codes[:].bitcast(FP8X4), scales=scales[:], in_=unit["grouped"][:])
+            parts = TILES if unit["by_tile"] else 1
+            width = BLOCKS * FEATURES // parts
+            for n in range(parts):
+                cols = slice(n * width // PACK, (n + 1) * width // PACK)
+                nc.vector.quantize_mx(
+                    out=codes[:, cols].bitcast(FP8X4),
+                    scales=scales[:, cols],
+                    in_=unit["grouped"][:, n * width : (n + 1) * width],
+                )
             unit["codes"] = codes
             unit["scales"] = scales
 
         def product(out, stationary, s_first, moving, m_first, m_width):
             for slot in range(SLOTS):
-                s_cols = slice(slot * WIDTH + s_first, slot * WIDTH + s_first + P)
+                first = s_first * SLOTS + slot * P if stationary["by_tile"] else slot * WIDTH + s_first
+                s_cols = slice(first, first + P)
                 m_cols = slice(slot * WIDTH + m_first, slot * WIDTH + m_first + m_width)
                 nc.tensor.matmul_mx(
                     out=out,
@@ -193,7 +237,10 @@ def tile_lstmcell_pb_kernel(
 
         def multiply_turned(number, t, half):
             unit = rounds[number]
-            bank = sums.tile([P, WIDTH], F32, name="sum")
+            if number == ROUNDS - 1 and t in [0]:
+                bank = transposed.tile([P, WIDTH], F32, name="bank")
+            else:
+                bank = sums.tile([P, WIDTH], F32, name="sum")
             product(bank[:], unit, t * P, halves[half], 0, WIDTH)
             unit.setdefault("sums", {})[t, half] = bank
 
@@ -233,12 +280,11 @@ def tile_lstmcell_pb_kernel(
             first = unit["part"] * WIDTH
             nc.sync.dma_start(out=out_h[:, rows, first + cols.start : first + cols.stop], in_=tile[:])
 
-        vector_blocks = [[3],[3],[],[],[],[],[],[],[],[]]
         for step in range(ROUNDS + 2):
             number = step - 3
             before = number - 1
             if step < len(units):
-                transpose_unit(units[step], vector_blocks[step])
+                transpose_unit(units[step], BLOCKS - 1 if step < HEAD_UNITS else 3 if step == len(units) - 1 else None)
             if step == 1:
                 for first in range(0, FIRST_TURNED * WIDTH, BANK):
                     bank = sums.tile([P, BANK], F32, name="sum")
@@ -270,7 +316,6 @@ def tile_lstmcell_pb_kernel(
                 for t in range(TILES):
                     for half in range(HALVES):
                         sigmoid_turned(number, t, half)
-
             if step < len(units):
                 quantise_unit(units[step], act_pool if step in (0, 2) else weight_pool)
             if 0 <= before < PARTS:
@@ -286,6 +331,8 @@ def tile_lstmcell_pb_kernel(
                 plus_g(before)
             if PARTS <= before < FIRST_TURNED:
                 times_tanh(before)
+            if step + 2 in ORDERED_UNITS:
+                order_words(units[step + 2])
 
         last = ROUNDS - 1
         before = last - 1
@@ -294,8 +341,8 @@ def tile_lstmcell_pb_kernel(
         for half in range(HALVES):
             for t in range(TILES):
                 turn(before, t, half)
-        multiply_turned(last, 1, 0)
-        multiply_turned(last, 1, 1)
+        for half in range(HALVES):
+            multiply_turned(last, 1, half)
         for t in range(TILES):
             for half in range(HALVES):
                 sigmoid_turned(last, t, half)

from contextlib import ExitStack

import concourse.mybir as mybir
from concourse.masks import make_identity

F32 = mybir.dt.float32
BF16 = mybir.dt.bfloat16
U32 = mybir.dt.uint32
U8 = mybir.dt.uint8
FP8X4 = mybir.dt.float8_e4m3fn_x4
ACT = mybir.ActivationFunctionType
ALU = mybir.AluOpType

P = 128
BATCH = 512
FEATURES = 1024
PACK = 4
K_PASS = P * PACK
PASSES = FEATURES // K_PASS
PAIRS = 2
SOURCES = 2
GATES = 2
BATCH_TILES = BATCH // P
WIDTH = 256
PARTS = FEATURES // WIDTH
ROUNDS = GATES * PARTS
HALVES = BATCH // WIDTH
TILES = WIDTH // P
BLOCKS = SOURCES * TILES
SLOTS = SOURCES * PASSES
HEAD_UNITS = 2
BIAS_UNIT = 1
C_UNIT = 5
G_UNIT = 5
BANK = 512
ORDERED_UNITS = (4, 5)
TURNED = 2
FIRST_TURNED = ROUNDS - TURNED

FLOPS = 2 * BATCH * (SOURCES * FEATURES) * (GATES * FEATURES)


def tile_lstmcell_pb_kernel(
    tc, incoming, h, c, gated_cand, W_f, b_W_f, W_o, b_W_o, U_f, b_U_f, U_o, b_U_o, out_0, out_1
):
    nc = tc.nc
    with ExitStack() as ctx:
        const = ctx.enter_context(tc.tile_pool(name="const", bufs=1))
        raw_pool = ctx.enter_context(tc.tile_pool(name="raw", bufs=1))
        ordered_pool = ctx.enter_context(tc.tile_pool(name="ordered", bufs=4))
        grouped_pool = ctx.enter_context(tc.tile_pool(name="grouped", bufs=3))
        act_pool = ctx.enter_context(tc.tile_pool(name="act", bufs=HALVES))
        weight_pool = ctx.enter_context(tc.tile_pool(name="weight", bufs=3))
        gate_pool = ctx.enter_context(tc.tile_pool(name="gate", bufs=4))
        turned_pool = ctx.enter_context(tc.tile_pool(name="turned", bufs=4))
        half_pool = ctx.enter_context(tc.tile_pool(name="half", bufs=6))
        cell_pool = ctx.enter_context(tc.tile_pool(name="cell", bufs=4))
        tanh_pool = ctx.enter_context(tc.tile_pool(name="tanh", bufs=4))
        transposed = ctx.enter_context(tc.psum_pool(name="transposed", bufs=4))
        sums = ctx.enter_context(tc.psum_pool(name="sums", bufs=4))
        ctx.enter_context(tc.manual_schedule())

        bias_rows = const.tile([P, GATES * FEATURES], BF16, name="bias_rows")
        nc.vector.memset(bias_rows[:].bitcast(U32), 0)
        ident = const.tile([P, P], F32, name="ident")
        make_identity(nc, ident[:])
        ones = const.tile([P, P], BF16, name="ones")
        nc.vector.memset(ones[:], 1.0)
        warm = const.tile([P, 1], F32, name="warm")
        nc.vector.memset(warm[:], 0.0)
        nc.scalar.activation(out=warm[:], in_=warm[:], func=ACT.Sigmoid)

        gate_weights = ((W_f, U_f), (W_o, U_o))
        x_rows, h_rows = (m.rearrange("(p b) k -> p b k", b=BATCH_TILES) for m in (incoming, h))
        halves = [{"loads": [m[:, a * TILES : (a + 1) * TILES, :] for m in (x_rows, h_rows)]} for a in range(HALVES)]
        rounds = []
        for number in range(ROUNDS):
            gate, part = divmod(number, PARTS)
            rows = slice(part * WIDTH, (part + 1) * WIDTH)
            view = "(t p) k -> p t k" if number == ROUNDS - 1 else "(p t) k -> p t k"
            loads = [m[rows, :].rearrange(view, t=TILES) for m in gate_weights[gate]]
            rounds.append({"loads": loads, "gate": gate, "part": part})
        units = [halves[0], rounds[0], halves[1]] + rounds[1:]

        for unit in units:
            unit["by_tile"] = unit is units[-1]

        c_sb = raw_pool.tile([P, BATCH_TILES, FEATURES], BF16, name="c_sb")
        g_sb = raw_pool.tile([P, BATCH_TILES, FEATURES], BF16, name="g_sb")
        for index, unit in enumerate(units):
            unit["raw"] = []
            unit["rows"] = []
            for a, rows in enumerate(unit["loads"]):
                raw = raw_pool.tile([P, TILES, FEATURES], BF16, name="raw_%d_%d" % (index, a))
                if index == 0 and a == 0:
                    for t in range(TILES):
                        nc.sync.dma_start(out=raw[:, t, :], in_=rows[:, t, :])
                else:
                    nc.sync.dma_start(out=raw[:], in_=rows)
                unit["rows"].append(raw)
                unit["raw"] += [raw[:, t, :] for t in range(TILES)]
            if index == BIAS_UNIT:
                for gate, pair in enumerate(((b_W_f, b_U_f), (b_W_o, b_U_o))):
                    for row, vector in enumerate(pair):
                        nc.scalar.dma_start(
                            out=bias_rows[row : row + 1, gate * FEATURES : (gate + 1) * FEATURES],
                            in_=vector.rearrange("(o n) -> o n", o=1),
                        )
            if index == C_UNIT:
                nc.sync.dma_start(out=c_sb[:], in_=c.rearrange("(p b) n -> p b n", b=BATCH_TILES))
            if index == G_UNIT:
                nc.sync.dma_start(out=g_sb[:], in_=gated_cand.rearrange("(p b) n -> p b n", b=BATCH_TILES))

        def order_words(unit):
            unit["ordered"] = []
            for raw in unit["rows"]:
                ordered = ordered_pool.tile([P, TILES, FEATURES], BF16, name="ordered")
                nc.vector.tensor_copy(
                    out=ordered[:].bitcast(F32).rearrange("p t (u w) -> p t u w", u=PAIRS),
                    in_=raw[:].bitcast(F32).rearrange("p t (w u) -> p t u w", u=PAIRS),
                )
                unit["ordered"] += [ordered[:, t, :] for t in range(TILES)]

        def transpose_unit(unit, vector_block):
            grouped = grouped_pool.tile([P, BLOCKS * FEATURES], BF16, name="grouped", align_bytes=64)
            grouped_words = grouped[:].bitcast(F32).rearrange("p (s r u) -> p s r u", s=SLOTS, u=PAIRS)
            if unit["by_tile"]:
                grouped_tiles = grouped[:].bitcast(F32).rearrange("p (t s r u) -> p t s r u", t=TILES, s=SLOTS, u=PAIRS)
            for n in range(BLOCKS):
                if unit["by_tile"]:
                    t, source = divmod(n, SOURCES)
                else:
                    source, t = divmod(n, TILES)
                i = source * TILES + t
                in_order = "ordered" in unit
                words = unit["ordered" if in_order else "raw"][i].bitcast(F32)
                bank = transposed.tile([P, PASSES, PAIRS, P], F32, name="bank")
                for g in range(PASSES):
                    for u in range(PAIRS):
                        if in_order:
                            picked = words[:, (u * PASSES + g) * P : (u * PASSES + g + 1) * P]
                        else:
                            picked = words[:, g * K_PASS // PAIRS + u : (g + 1) * K_PASS // PAIRS : PAIRS]
                        nc.tensor.transpose(bank[:, g, u, :], picked, ident[:])
                copy_out = nc.vector.tensor_copy if n == vector_block else nc.scalar.copy
                if unit["by_tile"]:
                    words_out = grouped_tiles[:, t, source * PASSES : (source + 1) * PASSES, :, :]
                else:
                    words_out = grouped_words[:, source * PASSES : (source + 1) * PASSES, t * P : (t + 1) * P, :]
                copy_out(
                    out=words_out,
                    in_=bank[:].rearrange("p g u r -> p g r u"),
                )
            unit["grouped"] = grouped

        def quantise_unit(unit, pool):
            codes = pool.tile([P, BLOCKS * FEATURES // PACK], U32, name="codes", align_bytes=64)
            scales = pool.tile([P, BLOCKS * FEATURES // PACK], U8, name="scales", align_bytes=64)
            parts = TILES if unit["by_tile"] else 1
            width = BLOCKS * FEATURES // parts
            for n in range(parts):
                cols = slice(n * width // PACK, (n + 1) * width // PACK)
                nc.vector.quantize_mx(
                    out=codes[:, cols].bitcast(FP8X4),
                    scales=scales[:, cols],
                    in_=unit["grouped"][:, n * width : (n + 1) * width],
                )
            unit["codes"] = codes
            unit["scales"] = scales

        def product(out, stationary, s_first, moving, m_first, m_width):
            for slot in range(SLOTS):
                first = s_first * SLOTS + slot * P if stationary["by_tile"] else slot * WIDTH + s_first
                s_cols = slice(first, first + P)
                m_cols = slice(slot * WIDTH + m_first, slot * WIDTH + m_first + m_width)
                nc.tensor.matmul_mx(
                    out=out,
                    lhsT=stationary["codes"][:, s_cols].bitcast(FP8X4),
                    lhsT_scale=stationary["scales"][:, s_cols],
                    rhs=moving["codes"][:, m_cols].bitcast(FP8X4),
                    rhs_scale=moving["scales"][:, m_cols],
                    start=(slot == 0),
                    stop=(slot == SLOTS - 1),
                )

        bias_sb = const.tile([P, FIRST_TURNED * WIDTH], F32, name="bias_sb")
        bias_turned = const.tile([P, TURNED * TILES], F32, name="bias_turned")
        out_h = out_0.rearrange("(p b) n -> p b n", b=BATCH_TILES)
        out_c = out_1.rearrange("(p b) n -> p b n", b=BATCH_TILES)

        def columns(number):
            part = rounds[number]["part"]
            return slice(part * WIDTH, (part + 1) * WIDTH)

        def multiply(number, half):
            bank = sums.tile([P, TILES, WIDTH], F32, name="sum")
            for j in range(TILES):
                product(bank[:, j, :], halves[half], j * P, rounds[number], 0, WIDTH)
            rounds[number].setdefault("sums", {})[half] = bank

        def add_bias(number, half):
            unit = rounds[number]
            if half == 0:
                unit["gate_tile"] = gate_pool.tile([P, BATCH_TILES, WIDTH], F32, name="gate")
            bias = bias_sb[:, number * WIDTH : (number + 1) * WIDTH].rearrange("p (r t) -> p r t", t=TILES)
            nc.vector.tensor_tensor(
                out=unit["gate_tile"][:, half * TILES : (half + 1) * TILES, :].rearrange("p j (r t) -> p j r t", t=TILES),
                in0=unit["sums"][half][:].rearrange("p j (t r) -> p j r t", t=TILES),
                in1=bias.unsqueeze(1).to_broadcast([P, TILES, WIDTH // TILES, TILES]),
                op=ALU.add,
            )

        def sigmoid(number):
            gate = rounds[number]["gate_tile"]
            nc.scalar.activation(out=gate[:], in_=gate[:], func=ACT.Sigmoid)

        def times_c(number):
            gate = rounds[number]["gate_tile"]
            nc.vector.tensor_tensor(out=gate[:], in0=gate[:], in1=c_sb[:, :, columns(number)], op=ALU.mult)

        def plus_g(number):
            cell = cell_pool.tile([P, BATCH_TILES, WIDTH], F32, name="cell")
            nc.vector.tensor_tensor(out=cell[:], in0=rounds[number]["gate_tile"][:], in1=g_sb[:, :, columns(number)], op=ALU.add)
            nc.sync.dma_start(out=out_c[:, :, columns(number)], in_=cell[:])
            rounds[number]["cell"] = cell

        def tanh(number):
            tile = tanh_pool.tile([P, BATCH_TILES, WIDTH], F32, name="tanh_c")
            nc.scalar.activation(out=tile[:], in_=rounds[number]["cell"][:], func=ACT.Tanh)
            rounds[number + PARTS]["tanh"] = tile

        def times_tanh(number):
            unit = rounds[number]
            gate = unit["gate_tile"]
            nc.vector.tensor_tensor(out=gate[:], in0=gate[:], in1=unit["tanh"][:], op=ALU.mult)
            nc.sync.dma_start(out=out_h[:, :, columns(number)], in_=gate[:])

        def multiply_turned(number, t, half):
            unit = rounds[number]
            if number == ROUNDS - 1 and t in [0]:
                bank = transposed.tile([P, WIDTH], F32, name="bank")
            else:
                bank = sums.tile([P, WIDTH], F32, name="sum")
            product(bank[:], unit, t * P, halves[half], 0, WIDTH)
            unit.setdefault("sums", {})[t, half] = bank

        def sigmoid_turned(number, t, half):
            unit = rounds[number]
            index = (number - FIRST_TURNED) * TILES + t
            tile = turned_pool.tile([P, WIDTH], F32, name="gate_t")
            nc.scalar.activation(out=tile[:], in_=unit["sums"][t, half][:], func=ACT.Sigmoid, bias=bias_turned[:, index : index + 1])
            unit.setdefault("gate_t", {})[t, half] = tile

        def turn(number, t, half):
            unit = rounds[number]
            together = number < ROUNDS - 1
            if t == 0 or not together:
                unit.setdefault("turned", {})[t, half] = transposed.tile([P, TILES, TILES if together else 1, P], F32, name="bank")
            bank = unit["turned"][0 if together else t, half]
            for j in range(TILES):
                nc.tensor.transpose(bank[:, j, t if together else 0, :], unit["gate_t"][t, half][:, j * P : (j + 1) * P], ident[:])

        def finish(number, half, t=None):
            unit = rounds[number]
            rows = slice(half * TILES, (half + 1) * TILES)
            bank = unit["turned"][0 if t is None else t, half]
            if t is None:
                cols = slice(0, WIDTH)
                in0 = bank[:].rearrange("p j t r -> p j r t")
            else:
                cols = slice(t * P, (t + 1) * P)
                in0 = bank[:, :, 0, :]
            tile = half_pool.tile([P, TILES, WIDTH if t is None else P], F32, name="hidden")
            out = tile[:]
            in1 = unit["tanh"][:, rows, cols]
            if t is None:
                out = out.rearrange("p j (r t) -> p j r t", t=TILES)
                in1 = in1.rearrange("p j (r t) -> p j r t", t=TILES)
            nc.vector.tensor_tensor(out=out, in0=in0, in1=in1, op=ALU.mult)
            first = unit["part"] * WIDTH
            nc.sync.dma_start(out=out_h[:, rows, first + cols.start : first + cols.stop], in_=tile[:])

        for step in range(ROUNDS + 2):
            number = step - 3
            before = number - 1
            if step < len(units):
                transpose_unit(units[step], BLOCKS - 1 if step < HEAD_UNITS else 3 if step == len(units) - 1 else None)
            if step == 1:
                for first in range(0, FIRST_TURNED * WIDTH, BANK):
                    bank = sums.tile([P, BANK], F32, name="sum")
                    nc.tensor.matmul(out=bank[:], lhsT=ones[:], rhs=bias_rows[:, first : first + BANK], start=True, stop=True)
                    nc.scalar.copy(out=bias_sb[:, first : first + BANK], in_=bank[:])
            if step == 2:
                bank = sums.tile([P, TURNED * TILES], F32, name="sum")
                for index in range(TURNED * TILES):
                    n, t = divmod(index, TILES)
                    first = (FIRST_TURNED + n) * WIDTH
                    cols = slice(first + t * P, first + (t + 1) * P) if FIRST_TURNED + n == ROUNDS - 1 else slice(first + t, first + WIDTH, TILES)
                    nc.tensor.matmul(out=bank[:, index : index + 1], lhsT=bias_rows[:, cols], rhs=ones[:, 0:1], start=True, stop=True)
                nc.scalar.copy(out=bias_turned[:], in_=bank[:])
            if 0 <= before < FIRST_TURNED:
                sigmoid(before)
            if 0 <= before - 1 < PARTS:
                tanh(before - 1)
            if step == 2:
                multiply(0, 0)
            if step == 3:
                multiply(0, 1)
            elif 1 <= number < FIRST_TURNED:
                for half in range(HALVES):
                    multiply(number, half)
            elif number >= FIRST_TURNED and number < ROUNDS - 1:
                for t in range(TILES):
                    for half in range(HALVES):
                        multiply_turned(number, t, half)
                for t in range(TILES):
                    for half in range(HALVES):
                        sigmoid_turned(number, t, half)
            if step < len(units):
                quantise_unit(units[step], act_pool if step in (0, 2) else weight_pool)
            if 0 <= before < PARTS:
                times_c(before)
            if step == 2:
                add_bias(0, 0)
            if step == 3:
                add_bias(0, 1)
            elif 1 <= number < FIRST_TURNED:
                for half in range(HALVES):
                    add_bias(number, half)
            if 0 <= before < PARTS:
                plus_g(before)
            if PARTS <= before < FIRST_TURNED:
                times_tanh(before)
            if step + 2 in ORDERED_UNITS:
                order_words(units[step + 2])

        last = ROUNDS - 1
        before = last - 1
        for half in range(HALVES):
            multiply_turned(last, 0, half)
        for half in range(HALVES):
            for t in range(TILES):
                turn(before, t, half)
        for half in range(HALVES):
            multiply_turned(last, 1, half)
        for t in range(TILES):
            for half in range(HALVES):
                sigmoid_turned(last, t, half)
        for half in range(HALVES):
            finish(before, half)
        for t in range(TILES):
            for half in range(HALVES):
                turn(last, t, half)
                finish(last, half, t)
